import numpy as np
import ml_dtypes


def mxq(x, axis, fmt="e4m3"):
    dtype, down = {"e4m3": (ml_dtypes.float8_e4m3fn, 7), "e5m2": (ml_dtypes.float8_e5m2, 14)}[fmt]
    v = np.moveaxis(np.asarray(x, np.float32).astype(ml_dtypes.bfloat16).astype(np.float64), axis, -1)
    blocks = v.reshape(v.shape[:-1] + (-1, 32))
    amax = np.abs(blocks).max(-1, keepdims=True)
    byte = np.maximum(np.where(amax > 0, np.frexp(amax)[1] - 1 + 127, 0) - down, 1)
    scale = np.exp2(byte - 127.0)
    codes = (blocks / scale).astype(np.float32).astype(dtype).astype(np.float64)
    return np.moveaxis((codes * scale).reshape(v.shape), -1, axis)


WIDE = False


def mx_kscale(k):
    if not WIDE:
        return np.ones(k)
    levels = np.array([10, -10, 5, -5, 0])
    if k % 512:
        return np.exp2(np.random.permutation(np.resize(levels, k // 32))).repeat(32)
    a = np.empty((k // 512, 16))
    for p in range(k // 512):
        a[p, :8] = np.random.permutation(np.resize(levels, 8))
        for g in range(8):
            far = levels[np.abs(levels - a[p, g]) >= 10]
            a[p, g + 8] = far[np.random.randint(len(far))]
    return np.exp2(a.ravel()).repeat(32)


BF16 = ml_dtypes.bfloat16


def bf(x):
    return np.asarray(x, np.float32).astype(BF16)


def f64(x):
    return np.asarray(x).astype(np.float64)


S, E, H, DH = 8192, 1024, 4, 32
W = H * DH


def rotate_half(t):
    return np.stack((-t[..., 1::2], t[..., ::2]), axis=-1).reshape(t.shape)


def setup_inputs():
    s = mx_kscale(E)
    return {"hidden_states": bf(np.random.standard_normal((S, E)) * s),
            "cos": bf(np.random.uniform(size=(S, DH))),
            "sin": bf(np.random.uniform(size=(S, DH))),
            "w_qkv": bf(np.random.standard_normal((E, 3 * W)) * 2.0 / np.sqrt(E) / s[:, None]),
            "b_qkv": bf(np.random.standard_normal(3 * W) * 0.3)}


def reference(hidden_states, cos, sin, w_qkv, b_qkv):
    qkv = ((mxq(f64(hidden_states), 1, "e4m3") @ mxq(f64(w_qkv), 0, "e4m3")) + f64(b_qkv)).reshape(S, 3, H, DH)
    q, k, v = qkv[:, 0], qkv[:, 1], qkv[:, 2]
    c = f64(cos)[:, None, :]
    sn = f64(sin)[:, None, :]
    q_rot = q * c + rotate_half(q) * sn
    k_rot = k * c + rotate_half(k) * sn
    return q_rot, k_rot, v

@@ -1,0 +1,291 @@
+from contextlib import ExitStack
+
+import concourse.mybir as mybir
+from concourse.masks import make_identity
+
+F32 = mybir.dt.float32
+BF16 = mybir.dt.bfloat16
+U32 = mybir.dt.uint32
+U8 = mybir.dt.uint8
+FP8X4 = mybir.dt.float8_e4m3fn_x4
+MULT = mybir.AluOpType.mult
+ADD = mybir.AluOpType.add
+IDENTITY = mybir.ActivationFunctionType.Identity
+
+P = 128
+PACK = 4
+TOKENS = 8192
+HIDDEN = 1024
+HEAD_DIM = 32
+PAIRS = HEAD_DIM // 2
+QK_HEADS = 8
+QK = QK_HEADS * HEAD_DIM
+HALF = QK // 2
+V = 4 * HEAD_DIM
+BANK = 512
+PASSES = HIDDEN // (P * PACK)
+WORD_BLOCKS = HIDDEN // (2 * P)
+TILES = TOKENS // P
+ROUND = 2
+ROUNDS = TILES // ROUND
+BLOCK = 4
+BLOCKS = TILES // BLOCK
+X_BUFS = 3
+TABLE_PARTS = {0: 16, 16: TILES}
+
+FLOPS = 2 * TOKENS * HIDDEN * (QK + V)
+
+
+def tile_arlowvisionattention_pa_t_kernel(
+    tc, hidden_states, cos, sin, w_qkv, b_qkv, out_0, out_1, out_2
+):
+    nc = tc.nc
+    x_view = hidden_states.rearrange("(p m) k -> p m k", m=TILES)
+    out_views = [o.rearrange("(p m) h d -> p m (h d)", m=TILES) for o in (out_0, out_1, out_2)]
+
+    with ExitStack() as ctx:
+        const = ctx.enter_context(tc.tile_pool(name="const", bufs=1))
+        x_pool = ctx.enter_context(tc.tile_pool(name="x", bufs=X_BUFS))
+        mx_pool = ctx.enter_context(tc.tile_pool(name="mx", bufs=3))
+        rope_pool = ctx.enter_context(tc.tile_pool(name="rope", bufs=3))
+        out_pool = ctx.enter_context(tc.tile_pool(name="out", bufs=3))
+        psum_x = ctx.enter_context(tc.psum_pool(name="psum_x", bufs=2))
+        psum_qk_t = ctx.enter_context(tc.psum_pool(name="psum_qk_t", bufs=2))
+        psum_qk = ctx.enter_context(tc.psum_pool(name="psum_qk", bufs=2))
+        psum_v = ctx.enter_context(tc.psum_pool(name="psum_v", bufs=2))
+        ctx.enter_context(tc.manual_schedule())
+
+        x_blocks = {}
+
+        def load_block(b, pieces):
+            x_blocks[b] = x_pool.tile([P, BLOCK, HIDDEN], BF16, name="x_blk")
+            step = BLOCK // pieces
+            for first in range(0, BLOCK, step):
+                nc.sync.dma_start(
+                    out=x_blocks[b][:, first : first + step, :],
+                    in_=x_view[:, b * BLOCK + first : b * BLOCK + first + step, :],
+                )
+
+        cos_sb = const.tile([P, TILES, HEAD_DIM], BF16, name="cos_sb")
+        sin_sb = const.tile([P, TILES, HEAD_DIM], BF16, name="sin_sb")
+
+        def load_tables(first, last):
+            for table_sb, table in ((cos_sb, cos), (sin_sb, sin)):
+                nc.sync.dma_start(
+                    out=table_sb[:, first:last, :],
+                    in_=table.rearrange("(p m) d -> p m d", m=TILES)[:, first:last, :],
+                )
+
+        bias_row = const.tile([P, BANK], BF16, name="bias_row")
+        nc.vector.memset(bias_row[:], 0.0)
+        nc.sync.dma_start(out=bias_row[0:1, 0 : QK + V], in_=b_qkv.rearrange("(o n) -> o n", o=1))
+        w_raw = const.tile([P, PASSES, PACK, QK + V], BF16, name="w_raw")
+        nc.sync.dma_start(
+            out=w_raw[:], in_=w_qkv.rearrange("(g p t) c -> p g t c", g=PASSES, t=PACK)
+        )
+        load_block(0, BLOCK // ROUND)
+        load_tables(0, TABLE_PARTS[0])
+        for b in range(1, X_BUFS):
+            load_block(b, 1)
+        load_tables(TABLE_PARTS[0], TILES)
+
+        ident_f32 = const.tile([P, P], F32, name="ident_f32")
+        make_identity(nc, ident_f32[:])
+        ident_bf16 = const.tile([P, P], BF16, name="ident_bf16")
+        make_identity(nc, ident_bf16[:])
+
+        ones = const.tile([P, P], BF16, name="ones")
+        nc.vector.memset(ones[:], 1.0)
+        bias_spread = psum_qk.tile([P, BANK], F32, name="bias_spread", tag="qk")
+        nc.tensor.matmul(out=bias_spread[:], lhsT=ones[:], rhs=bias_row[:], start=True, stop=True)
+        bias_v = const.tile([P, V], BF16, name="bias_v")
+        nc.scalar.copy(out=bias_v[:], in_=bias_spread[:, QK : QK + V])
+        bias_sorted = const.tile([P, 2, HALF], BF16, name="bias_sorted")
+        nc.vector.tensor_copy(
+            out=bias_sorted[:], in_=bias_row[:, 0:QK].rearrange("p (n e) -> p e n", e=2)
+        )
+        bias_sorted_t = psum_x.tile([P, 2, P], BF16, name="bias_sorted_t", tag="x_t")
+        for e in range(2):
+            nc.tensor.transpose(bias_sorted_t[:, e, :], bias_sorted[:, e, :], ident_bf16[:])
+        bias_qk = const.tile([P, 2], F32, name="bias_qk")
+        nc.scalar.copy(out=bias_qk[:], in_=bias_sorted_t[:, :, 0])
+
+        w_rows = w_raw[:]
+        w_halves = w_rows[:, :, :, 0:QK].rearrange("p g t (n e) -> p e g n t", e=2)
+        w_qk_grouped = const.tile([P, PASSES, 2, HALF, PACK], BF16, name="w_qk_grouped", align_bytes=64)
+        nc.vector.tensor_copy(out=w_qk_grouped[:, :, 0], in_=w_halves[:, 0])
+        nc.scalar.copy(out=w_qk_grouped[:, :, 1], in_=w_halves[:, 1])
+        w_v_grouped = const.tile([P, PASSES, V, PACK], BF16, name="w_v_grouped", align_bytes=64)
+        nc.vector.tensor_copy(
+            out=w_v_grouped[:], in_=w_rows[:, :, :, QK : QK + V].rearrange("p g t n -> p g n t")
+        )
+        w_qk_codes = const.tile([P, PASSES, 2, HALF], U32, name="w_qk_codes", align_bytes=64)
+        w_qk_scales = const.tile([P, PASSES, 2, HALF], U8, name="w_qk_scales", align_bytes=64)
+        nc.vector.quantize_mx(
+            out=w_qk_codes[:].rearrange("p g e n -> p (g e n)").bitcast(FP8X4),
+            scales=w_qk_scales[:].rearrange("p g e n -> p (g e n)"),
+            in_=w_qk_grouped[:].rearrange("p g e n t -> p (g e n t)"),
+        )
+        w_v_codes = const.tile([P, PASSES, V], U32, name="w_v_codes", align_bytes=64)
+        w_v_scales = const.tile([P, PASSES, V], U8, name="w_v_scales", align_bytes=64)
+        nc.vector.quantize_mx(
+            out=w_v_codes[:].rearrange("p g n -> p (g n)").bitcast(FP8X4),
+            scales=w_v_scales[:].rearrange("p g n -> p (g n)"),
+            in_=w_v_grouped[:].rearrange("p g n t -> p (g n t)"),
+        )
+
+        signs = const.tile([P, HEAD_DIM], BF16, name="signs")
+        nc.vector.memset(signs[:], 1.0)
+        nc.vector.memset(signs[:].rearrange("p (i e) -> p i e", e=2)[:, :, 0], -1.0)
+
+        def sign_sin(first, last):
+            nc.vector.tensor_tensor(
+                out=sin_sb[:, first:last, :],
+                in0=sin_sb[:, first:last, :],
+                in1=signs[:].unsqueeze(1).to_broadcast([P, last - first, HEAD_DIM]),
+                op=MULT,
+            )
+
+        def transpose_round(r):
+            grouped = mx_pool.tile([P, PASSES, ROUND, P, PACK], BF16, name="grouped", align_bytes=64)
+            grouped_words = grouped[:].bitcast(F32)
+            for a in range(ROUND):
+                tile_in_block = (r * ROUND + a) % BLOCK
+                words = x_blocks[r * ROUND // BLOCK][:, tile_in_block, :].bitcast(F32)
+                x_t = psum_x.tile([P, WORD_BLOCKS, P], F32, name="x_t", tag="x_t")
+                for j in range(WORD_BLOCKS):
+                    g, u = divmod(j, 2)
+                    nc.tensor.transpose(
+                        x_t[:, j, :], words[:, 2 * P * g + u : 2 * P * (g + 1) : 2], ident_f32[:]
+                    )
+                nc.scalar.copy(
+                    out=grouped_words[:, :, a], in_=x_t[:].rearrange("p (g u) r -> p g r u", u=2)
+                )
+            if (r + 1) * ROUND % BLOCK == 0 and r * ROUND // BLOCK + X_BUFS < BLOCKS:
+                load_block(r * ROUND // BLOCK + X_BUFS, 1)
+            return grouped
+
+        def quantise_round(grouped):
+            codes = mx_pool.tile([P, PASSES, ROUND, P], U32, name="codes", align_bytes=64)
+            scales = mx_pool.tile([P, PASSES, ROUND, P], U8, name="scales", align_bytes=64)
+            nc.vector.quantize_mx(
+                out=codes[:].rearrange("p g a r -> p (g a r)").bitcast(FP8X4),
+                scales=scales[:].rearrange("p g a r -> p (g a r)"),
+                in_=grouped[:].rearrange("p g a r t -> p (g a r t)"),
+            )
+            return codes, scales
+
+        def project_round(codes_and_scales):
+            codes, scales = codes_and_scales
+            qk_t = psum_qk_t.tile([P, 2, ROUND * P], F32, name="qk_t")
+            for e in range(2):
+                for g in range(PASSES):
+                    nc.tensor.matmul_mx(
+                        out=qk_t[:, e, :],
+                        lhsT=w_qk_codes[:, g, e, :].bitcast(FP8X4),
+                        lhsT_scale=w_qk_scales[:, g, e, :],
+                        rhs=codes[:, g].rearrange("p a r -> p (a r)").bitcast(FP8X4),
+                        rhs_scale=scales[:, g].rearrange("p a r -> p (a r)"),
+                        start=(g == 0),
+                        stop=(g == PASSES - 1),
+                    )
+            v = psum_v.tile([P, ROUND, V], F32, name="v")
+            for a in range(ROUND):
+                for g in range(PASSES):
+                    nc.tensor.matmul_mx(
+                        out=v[:, a, :],
+                        lhsT=codes[:, g, a, :].bitcast(FP8X4),
+                        lhsT_scale=scales[:, g, a, :],
+                        rhs=w_v_codes[:, g, :].bitcast(FP8X4),
+                        rhs_scale=w_v_scales[:, g, :],
+                        start=(g == 0),
+                        stop=(g == PASSES - 1),
+                    )
+            qk_t_sb = rope_pool.tile([P, 2, ROUND * P], F32, name="qk_t_sb")
+            for e in range(2):
+                nc.scalar.activation(
+                    out=qk_t_sb[:, e, :],
+                    in_=qk_t[:, e, :],
+                    func=IDENTITY,
+                    bias=bias_qk[:, e : e + 1],
+                    scale=1.0,
+                )
+            return qk_t_sb, v
+
+        def turn_back_round(qk_t_sb):
+            qk = psum_qk.tile([P, ROUND, 2, HALF], F32, name="qk", tag="qk")
+            for a in range(ROUND):
+                for e in range(2):
+                    nc.tensor.transpose(
+                        qk[:, a, e, :], qk_t_sb[:, e, a * P : (a + 1) * P], ident_f32[:]
+                    )
+            return qk
+
+        def multiply_round(r, qk):
+            shape = [P, ROUND, QK_HEADS, PAIRS, 2]
+            tiles = slice(r * ROUND, (r + 1) * ROUND)
+            halves = qk[:].rearrange("p a e (h i) -> p a e h i", i=PAIRS)
+            by_cos = rope_pool.tile(shape, F32, name="by_cos")
+            nc.vector.tensor_tensor(
+                out=by_cos[:],
+                in0=halves.rearrange("p a e h i -> p a h i e"),
+                in1=cos_sb[:, tiles, :].rearrange("p a (i e) -> p a i e", e=2).unsqueeze(2).to_broadcast(shape),
+                op=MULT,
+            )
+            by_sin = rope_pool.tile(shape, F32, name="by_sin")
+            nc.vector.tensor_tensor(
+                out=by_sin[:],
+                in0=halves[:, :, ::-1].rearrange("p a e h i -> p a h i e"),
+                in1=sin_sb[:, tiles, :].rearrange("p a (i e) -> p a i e", e=2).unsqueeze(2).to_broadcast(shape),
+                op=MULT,
+            )
+            return by_cos, by_sin
+
+        def finish_qk_round(r, by_cos, by_sin, out_blk):
+            first = r * ROUND % BLOCK
+            nc.gpsimd.tensor_tensor(
+                out=out_blk[:, 0:2, first : first + ROUND, :],
+                in0=by_cos[:].rearrange("p a (j h) i e -> p j a (h i e)", j=2),
+                in1=by_sin[:].rearrange("p a (j h) i e -> p j a (h i e)", j=2),
+                op=ADD,
+            )
+
+        def finish_v_round(r, v, out_blk):
+            first = r * ROUND % BLOCK
+            nc.vector.tensor_tensor(
+                out=out_blk[:, 2, first : first + ROUND, :],
+                in0=v[:],
+                in1=bias_v[:].unsqueeze(1).to_broadcast([P, ROUND, V]),
+                op=ADD,
+            )
+
+        quantised, projected, turned_back, out_blks = {}, {}, {}, {}
+        for r in range(-3, ROUNDS):
+            grouped = None
+            if r + 3 < ROUNDS:
+                grouped = transpose_round(r + 3)
+            if 0 <= r + 1 < ROUNDS:
+                turned_back[r + 1] = turn_back_round(projected[r + 1][0])
+            if 0 <= r + 2 < ROUNDS:
+                projected[r + 2] = project_round(quantised[r + 2])
+            if (r + 1) * ROUND in TABLE_PARTS:
+                sign_sin((r + 1) * ROUND, TABLE_PARTS[(r + 1) * ROUND])
+            if r >= 0:
+                by_cos, by_sin = multiply_round(r, turned_back[r])
+            if r + 3 < ROUNDS:
+                quantised[r + 3] = quantise_round(grouped)
+            if 0 <= r + 1 < ROUNDS:
+                if (r + 1) * ROUND % BLOCK == 0:
+                    out_blks[(r + 1) * ROUND // BLOCK] = out_pool.tile(
+                        [P, 3, BLOCK, V], F32, name="out_blk"
+                    )
+                finish_v_round(r + 1, projected[r + 1][1], out_blks[(r + 1) * ROUND // BLOCK])
+            if r >= 0:
+                b = r * ROUND // BLOCK
+                finish_qk_round(r, by_cos, by_sin, out_blks[b])
+                if (r + 1) * ROUND % BLOCK == 0:
+                    for j in range(3):
+                        nc.sync.dma_start(
+                            out=out_views[j][:, b * BLOCK : (b + 1) * BLOCK, :],
+                            in_=out_blks[b][:, j, :, :],
+                        )

@@ -48,7 +48,7 @@ def tile_arlowvisionattention_pa_t_kernel(
         x_pool = ctx.enter_context(tc.tile_pool(name="x", bufs=X_BUFS))
         mx_pool = ctx.enter_context(tc.tile_pool(name="mx", bufs=3))
         rope_pool = ctx.enter_context(tc.tile_pool(name="rope", bufs=3))
-        out_pool = ctx.enter_context(tc.tile_pool(name="out", bufs=3))
+        out_pool = ctx.enter_context(tc.tile_pool(name="out", bufs=4))
         psum_x = ctx.enter_context(tc.psum_pool(name="psum_x", bufs=2))
         psum_qk_t = ctx.enter_context(tc.psum_pool(name="psum_qk_t", bufs=2))
         psum_qk = ctx.enter_context(tc.psum_pool(name="psum_qk", bufs=2))
@@ -259,31 +259,30 @@ def tile_arlowvisionattention_pa_t_kernel(
                 op=ADD,
             )
 
-        quantised, projected, turned_back, out_blks = {}, {}, {}, {}
-        for r in range(-3, ROUNDS):
-            grouped = None
-            if r + 3 < ROUNDS:
-                grouped = transpose_round(r + 3)
-            if 0 <= r + 1 < ROUNDS:
-                turned_back[r + 1] = turn_back_round(projected[r + 1][0])
+        grouped_tiles, quantised, projected, turned_back, out_blks = {}, {}, {}, {}, {}
+        for r in range(-4, ROUNDS + 1):
+            if r + 4 < ROUNDS:
+                grouped_tiles[r + 4] = transpose_round(r + 4)
+            if 0 <= r < ROUNDS:
+                turned_back[r] = turn_back_round(projected[r][0])
             if 0 <= r + 2 < ROUNDS:
                 projected[r + 2] = project_round(quantised[r + 2])
-            if (r + 1) * ROUND in TABLE_PARTS:
-                sign_sin((r + 1) * ROUND, TABLE_PARTS[(r + 1) * ROUND])
-            if r >= 0:
-                by_cos, by_sin = multiply_round(r, turned_back[r])
-            if r + 3 < ROUNDS:
-                quantised[r + 3] = quantise_round(grouped)
+            if r * ROUND in TABLE_PARTS:
+                sign_sin(r * ROUND, TABLE_PARTS[r * ROUND])
+            if r >= 1:
+                by_cos, by_sin = multiply_round(r - 1, turned_back[r - 1])
+            if 0 <= r + 3 < ROUNDS:
+                quantised[r + 3] = quantise_round(grouped_tiles[r + 3])
             if 0 <= r + 1 < ROUNDS:
                 if (r + 1) * ROUND % BLOCK == 0:
                     out_blks[(r + 1) * ROUND // BLOCK] = out_pool.tile(
                         [P, 3, BLOCK, V], F32, name="out_blk"
                     )
                 finish_v_round(r + 1, projected[r + 1][1], out_blks[(r + 1) * ROUND // BLOCK])
-            if r >= 0:
-                b = r * ROUND // BLOCK
-                finish_qk_round(r, by_cos, by_sin, out_blks[b])
-                if (r + 1) * ROUND % BLOCK == 0:
+            if r >= 1:
+                b = (r - 1) * ROUND // BLOCK
+                finish_qk_round(r - 1, by_cos, by_sin, out_blks[b])
+                if r * ROUND % BLOCK == 0:
                     for j in range(3):
                         nc.sync.dma_start(
                             out=out_views[j][:, b * BLOCK : (b + 1) * BLOCK, :],

@@ -46,13 +46,13 @@ def tile_arlowvisionattention_pa_t_kernel(
     with ExitStack() as ctx:
         const = ctx.enter_context(tc.tile_pool(name="const", bufs=1))
         x_pool = ctx.enter_context(tc.tile_pool(name="x", bufs=X_BUFS))
-        mx_pool = ctx.enter_context(tc.tile_pool(name="mx", bufs=3))
-        rope_pool = ctx.enter_context(tc.tile_pool(name="rope", bufs=3))
+        mx_pool = ctx.enter_context(tc.tile_pool(name="mx", bufs=5))
+        rope_pool = ctx.enter_context(tc.tile_pool(name="rope", bufs=4))
         out_pool = ctx.enter_context(tc.tile_pool(name="out", bufs=4))
-        psum_x = ctx.enter_context(tc.psum_pool(name="psum_x", bufs=2))
+        psum_x = ctx.enter_context(tc.psum_pool(name="psum_x", bufs=3))
         psum_qk_t = ctx.enter_context(tc.psum_pool(name="psum_qk_t", bufs=2))
         psum_qk = ctx.enter_context(tc.psum_pool(name="psum_qk", bufs=2))
-        psum_v = ctx.enter_context(tc.psum_pool(name="psum_v", bufs=2))
+        psum_v = ctx.enter_context(tc.psum_pool(name="psum_v", bufs=1))
         ctx.enter_context(tc.manual_schedule())
 
         x_blocks = {}
@@ -175,7 +175,7 @@ def tile_arlowvisionattention_pa_t_kernel(
             )
             return codes, scales
 
-        def project_round(codes_and_scales):
+        def project_round(r, codes_and_scales, v):
             codes, scales = codes_and_scales
             qk_t = psum_qk_t.tile([P, 2, ROUND * P], F32, name="qk_t")
             for e in range(2):
@@ -189,11 +189,10 @@ def tile_arlowvisionattention_pa_t_kernel(
                         start=(g == 0),
                         stop=(g == PASSES - 1),
                     )
-            v = psum_v.tile([P, ROUND, V], F32, name="v")
             for a in range(ROUND):
                 for g in range(PASSES):
                     nc.tensor.matmul_mx(
-                        out=v[:, a, :],
+                        out=v[:, r * ROUND % BLOCK + a, :],
                         lhsT=codes[:, g, a, :].bitcast(FP8X4),
                         lhsT_scale=scales[:, g, a, :],
                         rhs=w_v_codes[:, g, :].bitcast(FP8X4),
@@ -210,7 +209,7 @@ def tile_arlowvisionattention_pa_t_kernel(
                     bias=bias_qk[:, e : e + 1],
                     scale=1.0,
                 )
-            return qk_t_sb, v
+            return qk_t_sb
 
         def turn_back_round(qk_t_sb):
             qk = psum_qk.tile([P, ROUND, 2, HALF], F32, name="qk", tag="qk")
@@ -250,41 +249,41 @@ def tile_arlowvisionattention_pa_t_kernel(
                 op=ADD,
             )
 
-        def finish_v_round(r, v, out_blk):
-            first = r * ROUND % BLOCK
+        def finish_v_block(v, out_blk):
             nc.vector.tensor_tensor(
-                out=out_blk[:, 2, first : first + ROUND, :],
+                out=out_blk[:, 2, :, :],
                 in0=v[:],
-                in1=bias_v[:].unsqueeze(1).to_broadcast([P, ROUND, V]),
+                in1=bias_v[:].unsqueeze(1).to_broadcast([P, BLOCK, V]),
                 op=ADD,
             )
 
         grouped_tiles, quantised, projected, turned_back, out_blks = {}, {}, {}, {}, {}
-        for r in range(-4, ROUNDS + 1):
-            if r + 4 < ROUNDS:
-                grouped_tiles[r + 4] = transpose_round(r + 4)
-            if 0 <= r < ROUNDS:
-                turned_back[r] = turn_back_round(projected[r][0])
-            if 0 <= r + 2 < ROUNDS:
-                projected[r + 2] = project_round(quantised[r + 2])
-            if r * ROUND in TABLE_PARTS:
-                sign_sin(r * ROUND, TABLE_PARTS[r * ROUND])
-            if r >= 1:
-                by_cos, by_sin = multiply_round(r - 1, turned_back[r - 1])
-            if 0 <= r + 3 < ROUNDS:
-                quantised[r + 3] = quantise_round(grouped_tiles[r + 3])
-            if 0 <= r + 1 < ROUNDS:
-                if (r + 1) * ROUND % BLOCK == 0:
-                    out_blks[(r + 1) * ROUND // BLOCK] = out_pool.tile(
-                        [P, 3, BLOCK, V], F32, name="out_blk"
+        for a in range(-4, ROUNDS, 2):
+            for r in (a, a + 1):
+                if r + 4 < ROUNDS:
+                    grouped_tiles[r + 4] = transpose_round(r + 4)
+                if r >= 0:
+                    turned_back[r] = turn_back_round(projected[r])
+            if 0 <= a + 2 < ROUNDS:
+                v = psum_v.tile([P, BLOCK, V], F32, name="v")
+                for r in (a + 2, a + 3):
+                    projected[r] = project_round(r, quantised[r], v)
+            if a * ROUND in TABLE_PARTS:
+                sign_sin(a * ROUND, TABLE_PARTS[a * ROUND])
+            for r in (a, a + 1):
+                if r >= 0:
+                    by_cos, by_sin = multiply_round(r, turned_back[r])
+                if r + 4 < ROUNDS:
+                    quantised[r + 4] = quantise_round(grouped_tiles[r + 4])
+                if r >= 0:
+                    finish_qk_round(r, by_cos, by_sin, out_blks[r * ROUND // BLOCK])
+            if 0 <= a + 2 < ROUNDS:
+                out_blks[(a + 2) * ROUND // BLOCK] = out_pool.tile([P, 3, BLOCK, V], F32, name="out_blk")
+                finish_v_block(v, out_blks[(a + 2) * ROUND // BLOCK])
+            if a >= 0:
+                b = a * ROUND // BLOCK
+                for j in range(3):
+                    nc.sync.dma_start(
+                        out=out_views[j][:, b * BLOCK : (b + 1) * BLOCK, :],
+                        in_=out_blks[b][:, j, :, :],
                     )
-                finish_v_round(r + 1, projected[r + 1][1], out_blks[(r + 1) * ROUND // BLOCK])
-            if r >= 1:
-                b = (r - 1) * ROUND // BLOCK
-                finish_qk_round(r - 1, by_cos, by_sin, out_blks[b])
-                if r * ROUND % BLOCK == 0:
-                    for j in range(3):
-                        nc.sync.dma_start(
-                            out=out_views[j][:, b * BLOCK : (b + 1) * BLOCK, :],
-                            in_=out_blks[b][:, j, :, :],
-                        )

@@ -31,6 +31,8 @@ ROUNDS = TILES // ROUND
 BLOCK = 4
 BLOCKS = TILES // BLOCK
 X_BUFS = 3
+FIRST_BLOCKS = 2
+FIRST_ROUNDS = FIRST_BLOCKS * BLOCK // ROUND
 TABLE_PARTS = {0: 16, 16: TILES}
 
 FLOPS = 2 * TOKENS * HIDDEN * (QK + V)
@@ -45,6 +47,7 @@ def tile_arlowvisionattention_pa_t_kernel(
 
     with ExitStack() as ctx:
         const = ctx.enter_context(tc.tile_pool(name="const", bufs=1))
+        x_first_pool = ctx.enter_context(tc.tile_pool(name="x_first", bufs=FIRST_ROUNDS))
         x_pool = ctx.enter_context(tc.tile_pool(name="x", bufs=X_BUFS))
         mx_pool = ctx.enter_context(tc.tile_pool(name="mx", bufs=5))
         rope_pool = ctx.enter_context(tc.tile_pool(name="rope", bufs=4))
@@ -55,16 +58,13 @@ def tile_arlowvisionattention_pa_t_kernel(
         psum_v = ctx.enter_context(tc.psum_pool(name="psum_v", bufs=1))
         ctx.enter_context(tc.manual_schedule())
 
-        x_blocks = {}
+        x_tiles = {}
 
-        def load_block(b, pieces):
-            x_blocks[b] = x_pool.tile([P, BLOCK, HIDDEN], BF16, name="x_blk")
-            step = BLOCK // pieces
-            for first in range(0, BLOCK, step):
-                nc.sync.dma_start(
-                    out=x_blocks[b][:, first : first + step, :],
-                    in_=x_view[:, b * BLOCK + first : b * BLOCK + first + step, :],
-                )
+        def load_tiles(pool, name, first, count):
+            x_sb = pool.tile([P, count, HIDDEN], BF16, name=name)
+            nc.sync.dma_start(out=x_sb[:], in_=x_view[:, first : first + count, :])
+            for i in range(count):
+                x_tiles[first + i] = (x_sb, i)
 
         cos_sb = const.tile([P, TILES, HEAD_DIM], BF16, name="cos_sb")
         sin_sb = const.tile([P, TILES, HEAD_DIM], BF16, name="sin_sb")
@@ -80,13 +80,15 @@ def tile_arlowvisionattention_pa_t_kernel(
         nc.vector.memset(bias_row[:], 0.0)
         nc.sync.dma_start(out=bias_row[0:1, 0 : QK + V], in_=b_qkv.rearrange("(o n) -> o n", o=1))
         w_raw = const.tile([P, PASSES, PACK, QK + V], BF16, name="w_raw")
-        nc.sync.dma_start(
-            out=w_raw[:], in_=w_qkv.rearrange("(g p t) c -> p g t c", g=PASSES, t=PACK)
-        )
-        load_block(0, BLOCK // ROUND)
+        for r in range(FIRST_ROUNDS):
+            if r == FIRST_ROUNDS // 2:
+                nc.sync.dma_start(
+                    out=w_raw[:], in_=w_qkv.rearrange("(g p t) c -> p g t c", g=PASSES, t=PACK)
+                )
+            load_tiles(x_first_pool, "x_round", r * ROUND, ROUND)
         load_tables(0, TABLE_PARTS[0])
-        for b in range(1, X_BUFS):
-            load_block(b, 1)
+        for b in range(FIRST_BLOCKS, FIRST_BLOCKS + X_BUFS):
+            load_tiles(x_pool, "x_blk", b * BLOCK, BLOCK)
         load_tables(TABLE_PARTS[0], TILES)
 
         ident_f32 = const.tile([P, P], F32, name="ident_f32")
@@ -110,29 +112,31 @@ def tile_arlowvisionattention_pa_t_kernel(
         bias_qk = const.tile([P, 2], F32, name="bias_qk")
         nc.scalar.copy(out=bias_qk[:], in_=bias_sorted_t[:, :, 0])
 
-        w_rows = w_raw[:]
-        w_halves = w_rows[:, :, :, 0:QK].rearrange("p g t (n e) -> p e g n t", e=2)
         w_qk_grouped = const.tile([P, PASSES, 2, HALF, PACK], BF16, name="w_qk_grouped", align_bytes=64)
-        nc.vector.tensor_copy(out=w_qk_grouped[:, :, 0], in_=w_halves[:, 0])
-        nc.scalar.copy(out=w_qk_grouped[:, :, 1], in_=w_halves[:, 1])
         w_v_grouped = const.tile([P, PASSES, V, PACK], BF16, name="w_v_grouped", align_bytes=64)
-        nc.vector.tensor_copy(
-            out=w_v_grouped[:], in_=w_rows[:, :, :, QK : QK + V].rearrange("p g t n -> p g n t")
-        )
         w_qk_codes = const.tile([P, PASSES, 2, HALF], U32, name="w_qk_codes", align_bytes=64)
         w_qk_scales = const.tile([P, PASSES, 2, HALF], U8, name="w_qk_scales", align_bytes=64)
-        nc.vector.quantize_mx(
-            out=w_qk_codes[:].rearrange("p g e n -> p (g e n)").bitcast(FP8X4),
-            scales=w_qk_scales[:].rearrange("p g e n -> p (g e n)"),
-            in_=w_qk_grouped[:].rearrange("p g e n t -> p (g e n t)"),
-        )
         w_v_codes = const.tile([P, PASSES, V], U32, name="w_v_codes", align_bytes=64)
         w_v_scales = const.tile([P, PASSES, V], U8, name="w_v_scales", align_bytes=64)
-        nc.vector.quantize_mx(
-            out=w_v_codes[:].rearrange("p g n -> p (g n)").bitcast(FP8X4),
-            scales=w_v_scales[:].rearrange("p g n -> p (g n)"),
-            in_=w_v_grouped[:].rearrange("p g n t -> p (g n t)"),
-        )
+
+        def prepare_weights():
+            w_rows = w_raw[:]
+            w_halves = w_rows[:, :, :, 0:QK].rearrange("p g t (n e) -> p e g n t", e=2)
+            nc.vector.tensor_copy(out=w_qk_grouped[:, :, 0], in_=w_halves[:, 0])
+            nc.scalar.copy(out=w_qk_grouped[:, :, 1], in_=w_halves[:, 1])
+            nc.vector.tensor_copy(
+                out=w_v_grouped[:], in_=w_rows[:, :, :, QK : QK + V].rearrange("p g t n -> p g n t")
+            )
+            nc.vector.quantize_mx(
+                out=w_qk_codes[:].rearrange("p g e n -> p (g e n)").bitcast(FP8X4),
+                scales=w_qk_scales[:].rearrange("p g e n -> p (g e n)"),
+                in_=w_qk_grouped[:].rearrange("p g e n t -> p (g e n t)"),
+            )
+            nc.vector.quantize_mx(
+                out=w_v_codes[:].rearrange("p g n -> p (g n)").bitcast(FP8X4),
+                scales=w_v_scales[:].rearrange("p g n -> p (g n)"),
+                in_=w_v_grouped[:].rearrange("p g n t -> p (g n t)"),
+            )
 
         signs = const.tile([P, HEAD_DIM], BF16, name="signs")
         nc.vector.memset(signs[:], 1.0)
@@ -150,8 +154,8 @@ def tile_arlowvisionattention_pa_t_kernel(
             grouped = mx_pool.tile([P, PASSES, ROUND, P, PACK], BF16, name="grouped", align_bytes=64)
             grouped_words = grouped[:].bitcast(F32)
             for a in range(ROUND):
-                tile_in_block = (r * ROUND + a) % BLOCK
-                words = x_blocks[r * ROUND // BLOCK][:, tile_in_block, :].bitcast(F32)
+                x_sb, place = x_tiles[r * ROUND + a]
+                words = x_sb[:, place, :].bitcast(F32)
                 x_t = psum_x.tile([P, WORD_BLOCKS, P], F32, name="x_t", tag="x_t")
                 for j in range(WORD_BLOCKS):
                     g, u = divmod(j, 2)
@@ -161,8 +165,9 @@ def tile_arlowvisionattention_pa_t_kernel(
                 nc.scalar.copy(
                     out=grouped_words[:, :, a], in_=x_t[:].rearrange("p (g u) r -> p g r u", u=2)
                 )
-            if (r + 1) * ROUND % BLOCK == 0 and r * ROUND // BLOCK + X_BUFS < BLOCKS:
-                load_block(r * ROUND // BLOCK + X_BUFS, 1)
+            b = r * ROUND // BLOCK
+            if (r + 1) * ROUND % BLOCK == 0 and FIRST_BLOCKS <= b < BLOCKS - X_BUFS:
+                load_tiles(x_pool, "x_blk", (b + X_BUFS) * BLOCK, BLOCK)
             return grouped
 
         def quantise_round(grouped):
@@ -240,9 +245,9 @@ def tile_arlowvisionattention_pa_t_kernel(
             )
             return by_cos, by_sin
 
-        def finish_qk_round(r, by_cos, by_sin, out_blk):
+        def finish_qk_round(engine, r, by_cos, by_sin, out_blk):
             first = r * ROUND % BLOCK
-            nc.gpsimd.tensor_tensor(
+            engine.tensor_tensor(
                 out=out_blk[:, 0:2, first : first + ROUND, :],
                 in0=by_cos[:].rearrange("p a (j h) i e -> p j a (h i e)", j=2),
                 in1=by_sin[:].rearrange("p a (j h) i e -> p j a (h i e)", j=2),
@@ -258,6 +263,15 @@ def tile_arlowvisionattention_pa_t_kernel(
             )
 
         grouped_tiles, quantised, projected, turned_back, out_blks = {}, {}, {}, {}, {}
+
+        def store(outputs, first, count):
+            place = first % BLOCK
+            for j in outputs:
+                nc.sync.dma_start(
+                    out=out_views[j][:, first : first + count, :],
+                    in_=out_blks[first // BLOCK][:, j, place : place + count, :],
+                )
+
         for a in range(-4, ROUNDS, 2):
             for r in (a, a + 1):
                 if r + 4 < ROUNDS:
@@ -276,14 +290,15 @@ def tile_arlowvisionattention_pa_t_kernel(
                 if r + 4 < ROUNDS:
                     quantised[r + 4] = quantise_round(grouped_tiles[r + 4])
                 if r >= 0:
-                    finish_qk_round(r, by_cos, by_sin, out_blks[r * ROUND // BLOCK])
+                    engine = nc.vector if r == ROUNDS - 1 else nc.gpsimd
+                    finish_qk_round(engine, r, by_cos, by_sin, out_blks[r * ROUND // BLOCK])
+                    if a == ROUNDS - 2:
+                        store(range(2), r * ROUND, ROUND)
+            if a == -4:
+                prepare_weights()
             if 0 <= a + 2 < ROUNDS:
                 out_blks[(a + 2) * ROUND // BLOCK] = out_pool.tile([P, 3, BLOCK, V], F32, name="out_blk")
                 finish_v_block(v, out_blks[(a + 2) * ROUND // BLOCK])
-            if a >= 0:
-                b = a * ROUND // BLOCK
-                for j in range(3):
-                    nc.sync.dma_start(
-                        out=out_views[j][:, b * BLOCK : (b + 1) * BLOCK, :],
-                        in_=out_blks[b][:, j, :, :],
-                    )
+                store(range(2, 3), (a + 2) * ROUND, BLOCK)
+            if 0 <= a < ROUNDS - 2:
+                store(range(2), a * ROUND, BLOCK)

@@ -78,10 +78,12 @@ def tile_arlowvisionattention_pa_t_kernel(
 
         bias_row = const.tile([P, BANK], BF16, name="bias_row")
         nc.vector.memset(bias_row[:], 0.0)
-        nc.sync.dma_start(out=bias_row[0:1, 0 : QK + V], in_=b_qkv.rearrange("(o n) -> o n", o=1))
         w_raw = const.tile([P, PASSES, PACK, QK + V], BF16, name="w_raw")
         for r in range(FIRST_ROUNDS):
             if r == FIRST_ROUNDS // 2:
+                nc.sync.dma_start(
+                    out=bias_row[0:1, 0 : QK + V], in_=b_qkv.rearrange("(o n) -> o n", o=1)
+                )
                 nc.sync.dma_start(
                     out=w_raw[:], in_=w_qkv.rearrange("(g p t) c -> p g t c", g=PASSES, t=PACK)
                 )
@@ -98,19 +100,22 @@ def tile_arlowvisionattention_pa_t_kernel(
 
         ones = const.tile([P, P], BF16, name="ones")
         nc.vector.memset(ones[:], 1.0)
-        bias_spread = psum_qk.tile([P, BANK], F32, name="bias_spread", tag="qk")
-        nc.tensor.matmul(out=bias_spread[:], lhsT=ones[:], rhs=bias_row[:], start=True, stop=True)
         bias_v = const.tile([P, V], BF16, name="bias_v")
-        nc.scalar.copy(out=bias_v[:], in_=bias_spread[:, QK : QK + V])
         bias_sorted = const.tile([P, 2, HALF], BF16, name="bias_sorted")
+        bias_qk = const.tile([P, 2], F32, name="bias_qk")
+
         nc.vector.tensor_copy(
             out=bias_sorted[:], in_=bias_row[:, 0:QK].rearrange("p (n e) -> p e n", e=2)
         )
-        bias_sorted_t = psum_x.tile([P, 2, P], BF16, name="bias_sorted_t", tag="x_t")
-        for e in range(2):
-            nc.tensor.transpose(bias_sorted_t[:, e, :], bias_sorted[:, e, :], ident_bf16[:])
-        bias_qk = const.tile([P, 2], F32, name="bias_qk")
-        nc.scalar.copy(out=bias_qk[:], in_=bias_sorted_t[:, :, 0])
+
+        def spread_bias():
+            bias_spread = psum_qk.tile([P, BANK], F32, name="bias_spread", tag="qk")
+            nc.tensor.matmul(out=bias_spread[:], lhsT=ones[:], rhs=bias_row[:], start=True, stop=True)
+            nc.scalar.copy(out=bias_v[:], in_=bias_spread[:, QK : QK + V])
+            bias_sorted_t = psum_x.tile([P, 2, P], BF16, name="bias_sorted_t", tag="x_t")
+            for e in range(2):
+                nc.tensor.transpose(bias_sorted_t[:, e, :], bias_sorted[:, e, :], ident_bf16[:])
+            nc.scalar.copy(out=bias_qk[:], in_=bias_sorted_t[:, :, 0])
 
         w_qk_grouped = const.tile([P, PASSES, 2, HALF, PACK], BF16, name="w_qk_grouped", align_bytes=64)
         w_v_grouped = const.tile([P, PASSES, V, PACK], BF16, name="w_v_grouped", align_bytes=64)
@@ -278,6 +283,8 @@ def tile_arlowvisionattention_pa_t_kernel(
                     grouped_tiles[r + 4] = transpose_round(r + 4)
                 if r >= 0:
                     turned_back[r] = turn_back_round(projected[r])
+            if a == -2:
+                spread_bias()
             if 0 <= a + 2 < ROUNDS:
                 v = psum_v.tile([P, BLOCK, V], F32, name="v")
                 for r in (a + 2, a + 3):

@@ -185,7 +185,7 @@ def tile_arlowvisionattention_pa_t_kernel(
             )
             return codes, scales
 
-        def project_round(r, codes_and_scales, v):
+        def project_qk_round(codes_and_scales):
             codes, scales = codes_and_scales
             qk_t = psum_qk_t.tile([P, 2, ROUND * P], F32, name="qk_t")
             for e in range(2):
@@ -199,6 +199,19 @@ def tile_arlowvisionattention_pa_t_kernel(
                         start=(g == 0),
                         stop=(g == PASSES - 1),
                     )
+            qk_t_sb = rope_pool.tile([P, 2, ROUND * P], F32, name="qk_t_sb")
+            for e in range(2):
+                nc.scalar.activation(
+                    out=qk_t_sb[:, e, :],
+                    in_=qk_t[:, e, :],
+                    func=IDENTITY,
+                    bias=bias_qk[:, e : e + 1],
+                    scale=1.0,
+                )
+            return qk_t_sb
+
+        def project_v_round(r, codes_and_scales, v):
+            codes, scales = codes_and_scales
             for a in range(ROUND):
                 for g in range(PASSES):
                     nc.tensor.matmul_mx(
@@ -210,16 +223,6 @@ def tile_arlowvisionattention_pa_t_kernel(
                         start=(g == 0),
                         stop=(g == PASSES - 1),
                     )
-            qk_t_sb = rope_pool.tile([P, 2, ROUND * P], F32, name="qk_t_sb")
-            for e in range(2):
-                nc.scalar.activation(
-                    out=qk_t_sb[:, e, :],
-                    in_=qk_t[:, e, :],
-                    func=IDENTITY,
-                    bias=bias_qk[:, e : e + 1],
-                    scale=1.0,
-                )
-            return qk_t_sb
 
         def turn_back_round(qk_t_sb):
             qk = psum_qk.tile([P, ROUND, 2, HALF], F32, name="qk", tag="qk")
@@ -283,12 +286,14 @@ def tile_arlowvisionattention_pa_t_kernel(
                     grouped_tiles[r + 4] = transpose_round(r + 4)
                 if r >= 0:
                     turned_back[r] = turn_back_round(projected[r])
-            if a == -2:
-                spread_bias()
+                if r == -2:
+                    spread_bias()
+                if 0 <= r + 2 < ROUNDS:
+                    projected[r + 2] = project_qk_round(quantised[r + 2])
             if 0 <= a + 2 < ROUNDS:
                 v = psum_v.tile([P, BLOCK, V], F32, name="v")
                 for r in (a + 2, a + 3):
-                    projected[r] = project_round(r, quantised[r], v)
+                    project_v_round(r, quantised[r], v)
             if a * ROUND in TABLE_PARTS:
                 sign_sin(a * ROUND, TABLE_PARTS[a * ROUND])
             for r in (a, a + 1):

@@ -49,6 +49,7 @@ def tile_arlowvisionattention_pa_t_kernel(
         const = ctx.enter_context(tc.tile_pool(name="const", bufs=1))
         x_first_pool = ctx.enter_context(tc.tile_pool(name="x_first", bufs=FIRST_ROUNDS))
         x_pool = ctx.enter_context(tc.tile_pool(name="x", bufs=X_BUFS))
+        sort_pool = ctx.enter_context(tc.tile_pool(name="sort", bufs=2))
         mx_pool = ctx.enter_context(tc.tile_pool(name="mx", bufs=5))
         rope_pool = ctx.enter_context(tc.tile_pool(name="rope", bufs=4))
         out_pool = ctx.enter_context(tc.tile_pool(name="out", bufs=4))
@@ -155,18 +156,32 @@ def tile_arlowvisionattention_pa_t_kernel(
                 op=MULT,
             )
 
+        sorted_tiles = {}
+
+        def sort_tile(tile_index):
+            x_sb, place = x_tiles[tile_index]
+            x_sorted = sort_pool.tile([P, PASSES, 2, P], F32, name="x_sorted")
+            nc.scalar.copy(
+                out=x_sorted[:],
+                in_=x_sb[:, place, :].bitcast(F32).rearrange("p (g w u) -> p g u w", g=PASSES, u=2),
+            )
+            sorted_tiles[tile_index] = x_sorted
+
         def transpose_round(r):
             grouped = mx_pool.tile([P, PASSES, ROUND, P, PACK], BF16, name="grouped", align_bytes=64)
             grouped_words = grouped[:].bitcast(F32)
             for a in range(ROUND):
                 x_sb, place = x_tiles[r * ROUND + a]
                 words = x_sb[:, place, :].bitcast(F32)
+                x_sorted = sorted_tiles.get(r * ROUND + a)
                 x_t = psum_x.tile([P, WORD_BLOCKS, P], F32, name="x_t", tag="x_t")
                 for j in range(WORD_BLOCKS):
                     g, u = divmod(j, 2)
-                    nc.tensor.transpose(
-                        x_t[:, j, :], words[:, 2 * P * g + u : 2 * P * (g + 1) : 2], ident_f32[:]
-                    )
+                    if x_sorted is None:
+                        every_2nd = words[:, 2 * P * g + u : 2 * P * (g + 1) : 2]
+                    else:
+                        every_2nd = x_sorted[:, g, u, :]
+                    nc.tensor.transpose(x_t[:, j, :], every_2nd, ident_f32[:])
                 nc.scalar.copy(
                     out=grouped_words[:, :, a], in_=x_t[:].rearrange("p (g u) r -> p g r u", u=2)
                 )
@@ -294,6 +309,8 @@ def tile_arlowvisionattention_pa_t_kernel(
                 v = psum_v.tile([P, BLOCK, V], F32, name="v")
                 for r in (a + 2, a + 3):
                     project_v_round(r, quantised[r], v)
+                if a + 6 < ROUNDS:
+                    sort_tile((a + 8) * ROUND - 1)
             if a * ROUND in TABLE_PARTS:
                 sign_sin(a * ROUND, TABLE_PARTS[a * ROUND])
             for r in (a, a + 1):

@@ -32,7 +32,7 @@ BLOCK = 4
 BLOCKS = TILES // BLOCK
 X_BUFS = 3
 FIRST_BLOCKS = 2
-FIRST_ROUNDS = FIRST_BLOCKS * BLOCK // ROUND
+FIRST_TILES = FIRST_BLOCKS * BLOCK
 TABLE_PARTS = {0: 16, 16: TILES}
 
 FLOPS = 2 * TOKENS * HIDDEN * (QK + V)
@@ -47,7 +47,7 @@ def tile_arlowvisionattention_pa_t_kernel(
 
     with ExitStack() as ctx:
         const = ctx.enter_context(tc.tile_pool(name="const", bufs=1))
-        x_first_pool = ctx.enter_context(tc.tile_pool(name="x_first", bufs=FIRST_ROUNDS))
+        x_first_pool = ctx.enter_context(tc.tile_pool(name="x_first", bufs=BLOCK))
         x_pool = ctx.enter_context(tc.tile_pool(name="x", bufs=X_BUFS))
         sort_pool = ctx.enter_context(tc.tile_pool(name="sort", bufs=2))
         mx_pool = ctx.enter_context(tc.tile_pool(name="mx", bufs=5))
@@ -80,15 +80,16 @@ def tile_arlowvisionattention_pa_t_kernel(
         bias_row = const.tile([P, BANK], BF16, name="bias_row")
         nc.vector.memset(bias_row[:], 0.0)
         w_raw = const.tile([P, PASSES, PACK, QK + V], BF16, name="w_raw")
-        for r in range(FIRST_ROUNDS):
-            if r == FIRST_ROUNDS // 2:
-                nc.sync.dma_start(
-                    out=bias_row[0:1, 0 : QK + V], in_=b_qkv.rearrange("(o n) -> o n", o=1)
-                )
-                nc.sync.dma_start(
-                    out=w_raw[:], in_=w_qkv.rearrange("(g p t) c -> p g t c", g=PASSES, t=PACK)
-                )
-            load_tiles(x_first_pool, "x_round", r * ROUND, ROUND)
+        nc.sync.dma_start(
+            out=w_raw[:], in_=w_qkv.rearrange("(g p t) c -> p g t c", g=PASSES, t=PACK)
+        )
+        nc.sync.dma_start(
+            out=bias_row[0:1, 0 : QK + V], in_=b_qkv.rearrange("(o n) -> o n", o=1)
+        )
+        for i in range(BLOCK):
+            load_tiles(x_first_pool, "x_tile", i, 1)
+        for i in range(BLOCK, FIRST_TILES, ROUND):
+            load_tiles(x_first_pool, "x_round", i, ROUND)
         load_tables(0, TABLE_PARTS[0])
         for b in range(FIRST_BLOCKS, FIRST_BLOCKS + X_BUFS):
             load_tiles(x_pool, "x_blk", b * BLOCK, BLOCK)
@@ -104,10 +105,6 @@ def tile_arlowvisionattention_pa_t_kernel(
         bias_v = const.tile([P, V], BF16, name="bias_v")
         bias_sorted = const.tile([P, 2, HALF], BF16, name="bias_sorted")
         bias_qk = const.tile([P, 2], F32, name="bias_qk")
-
-        nc.vector.tensor_copy(
-            out=bias_sorted[:], in_=bias_row[:, 0:QK].rearrange("p (n e) -> p e n", e=2)
-        )
 
         def spread_bias():
             bias_spread = psum_qk.tile([P, BANK], F32, name="bias_spread", tag="qk")
@@ -295,6 +292,11 @@ def tile_arlowvisionattention_pa_t_kernel(
                     in_=out_blks[first // BLOCK][:, j, place : place + count, :],
                 )
 
+        prepare_weights()
+        nc.vector.tensor_copy(
+            out=bias_sorted[:], in_=bias_row[:, 0:QK].rearrange("p (n e) -> p e n", e=2)
+        )
+
         for a in range(-4, ROUNDS, 2):
             for r in (a, a + 1):
                 if r + 4 < ROUNDS:
@@ -323,8 +325,6 @@ def tile_arlowvisionattention_pa_t_kernel(
                     finish_qk_round(engine, r, by_cos, by_sin, out_blks[r * ROUND // BLOCK])
                     if a == ROUNDS - 2:
                         store(range(2), r * ROUND, ROUND)
-            if a == -4:
-                prepare_weights()
             if 0 <= a + 2 < ROUNDS:
                 out_blks[(a + 2) * ROUND // BLOCK] = out_pool.tile([P, 3, BLOCK, V], F32, name="out_blk")
                 finish_v_block(v, out_blks[(a + 2) * ROUND // BLOCK])

@@ -159,8 +159,8 @@ def tile_arlowvisionattention_pa_t_kernel(
             x_sb, place = x_tiles[tile_index]
             x_sorted = sort_pool.tile([P, PASSES, 2, P], F32, name="x_sorted")
             nc.scalar.copy(
-                out=x_sorted[:],
-                in_=x_sb[:, place, :].bitcast(F32).rearrange("p (g w u) -> p g u w", g=PASSES, u=2),
+                out=x_sorted[:].rearrange("p g u w -> p g w u"),
+                in_=x_sb[:, place, :].bitcast(F32).rearrange("p (g w u) -> p g w u", g=PASSES, u=2),
             )
             sorted_tiles[tile_index] = x_sorted
 

@@ -47,7 +47,7 @@ def tile_arlowvisionattention_pa_t_kernel(
 
     with ExitStack() as ctx:
         const = ctx.enter_context(tc.tile_pool(name="const", bufs=1))
-        x_first_pool = ctx.enter_context(tc.tile_pool(name="x_first", bufs=BLOCK))
+        x_first_pool = ctx.enter_context(tc.tile_pool(name="x_first", bufs=FIRST_TILES))
         x_pool = ctx.enter_context(tc.tile_pool(name="x", bufs=X_BUFS))
         sort_pool = ctx.enter_context(tc.tile_pool(name="sort", bufs=2))
         mx_pool = ctx.enter_context(tc.tile_pool(name="mx", bufs=5))
@@ -86,10 +86,8 @@ def tile_arlowvisionattention_pa_t_kernel(
         nc.sync.dma_start(
             out=bias_row[0:1, 0 : QK + V], in_=b_qkv.rearrange("(o n) -> o n", o=1)
         )
-        for i in range(BLOCK):
+        for i in range(FIRST_TILES):
             load_tiles(x_first_pool, "x_tile", i, 1)
-        for i in range(BLOCK, FIRST_TILES, ROUND):
-            load_tiles(x_first_pool, "x_round", i, ROUND)
         load_tables(0, TABLE_PARTS[0])
         for b in range(FIRST_BLOCKS, FIRST_BLOCKS + X_BUFS):
             load_tiles(x_pool, "x_blk", b * BLOCK, BLOCK)
@@ -268,9 +266,9 @@ def tile_arlowvisionattention_pa_t_kernel(
         def finish_qk_round(engine, r, by_cos, by_sin, out_blk):
             first = r * ROUND % BLOCK
             engine.tensor_tensor(
-                out=out_blk[:, 0:2, first : first + ROUND, :],
-                in0=by_cos[:].rearrange("p a (j h) i e -> p j a (h i e)", j=2),
-                in1=by_sin[:].rearrange("p a (j h) i e -> p j a (h i e)", j=2),
+                out=out_blk[:, 0:2, first : first + ROUND, :].rearrange("p j a c -> p a j c"),
+                in0=by_cos[:].rearrange("p a (j h) i e -> p a j (h i e)", j=2),
+                in1=by_sin[:].rearrange("p a (j h) i e -> p a j (h i e)", j=2),
                 op=ADD,
             )
 

@@ -32,6 +32,7 @@ BLOCK = 4
 BLOCKS = TILES // BLOCK
 X_BUFS = 3
 FIRST_BLOCKS = 2
+V_TURNED = 2
 FIRST_TILES = FIRST_BLOCKS * BLOCK
 TABLE_PARTS = {0: 16, 16: TILES}
 
@@ -101,17 +102,17 @@ def tile_arlowvisionattention_pa_t_kernel(
         ones = const.tile([P, P], BF16, name="ones")
         nc.vector.memset(ones[:], 1.0)
         bias_v = const.tile([P, V], BF16, name="bias_v")
-        bias_sorted = const.tile([P, 2, HALF], BF16, name="bias_sorted")
-        bias_qk = const.tile([P, 2], F32, name="bias_qk")
+        bias_sorted = const.tile([P, 3, P], BF16, name="bias_sorted")
+        bias_cols = const.tile([P, 3], F32, name="bias_cols")
 
         def spread_bias():
             bias_spread = psum_qk.tile([P, BANK], F32, name="bias_spread", tag="qk")
             nc.tensor.matmul(out=bias_spread[:], lhsT=ones[:], rhs=bias_row[:], start=True, stop=True)
             nc.scalar.copy(out=bias_v[:], in_=bias_spread[:, QK : QK + V])
-            bias_sorted_t = psum_x.tile([P, 2, P], BF16, name="bias_sorted_t", tag="x_t")
-            for e in range(2):
+            bias_sorted_t = psum_x.tile([P, 3, P], BF16, name="bias_sorted_t", tag="x_t")
+            for e in range(3):
                 nc.tensor.transpose(bias_sorted_t[:, e, :], bias_sorted[:, e, :], ident_bf16[:])
-            nc.scalar.copy(out=bias_qk[:], in_=bias_sorted_t[:, :, 0])
+            nc.scalar.copy(out=bias_cols[:], in_=bias_sorted_t[:, :, 0])
 
         w_qk_grouped = const.tile([P, PASSES, 2, HALF, PACK], BF16, name="w_qk_grouped", align_bytes=64)
         w_v_grouped = const.tile([P, PASSES, V, PACK], BF16, name="w_v_grouped", align_bytes=64)
@@ -215,13 +216,25 @@ def tile_arlowvisionattention_pa_t_kernel(
                     out=qk_t_sb[:, e, :],
                     in_=qk_t[:, e, :],
                     func=IDENTITY,
-                    bias=bias_qk[:, e : e + 1],
+                    bias=bias_cols[:, e : e + 1],
                     scale=1.0,
                 )
             return qk_t_sb
 
         def project_v_round(r, codes_and_scales, v):
             codes, scales = codes_and_scales
+            if r * ROUND // BLOCK >= BLOCKS - V_TURNED:
+                for g in range(PASSES):
+                    nc.tensor.matmul_mx(
+                        out=v[:, r * ROUND % BLOCK : r * ROUND % BLOCK + ROUND, :].rearrange("p a c -> p (a c)"),
+                        lhsT=w_v_codes[:, g, :].bitcast(FP8X4),
+                        lhsT_scale=w_v_scales[:, g, :],
+                        rhs=codes[:, g].rearrange("p a r -> p (a r)").bitcast(FP8X4),
+                        rhs_scale=scales[:, g].rearrange("p a r -> p (a r)"),
+                        start=(g == 0),
+                        stop=(g == PASSES - 1),
+                    )
+                return
             for a in range(ROUND):
                 for g in range(PASSES):
                     nc.tensor.matmul_mx(
@@ -272,6 +285,19 @@ def tile_arlowvisionattention_pa_t_kernel(
                 op=ADD,
             )
 
+        def empty_v_block(v):
+            v_t_sb = rope_pool.tile([P, BLOCK, P], F32, name="v_t_sb")
+            nc.scalar.activation(
+                out=v_t_sb[:], in_=v[:], func=IDENTITY, bias=bias_cols[:, 2:3], scale=1.0
+            )
+            return v_t_sb
+
+        def turn_back_v_block(v_t_sb, out_blk):
+            v_back = psum_x.tile([P, BLOCK, P], F32, name="v_back", tag="x_t")
+            for i in range(BLOCK):
+                nc.tensor.transpose(v_back[:, i, :], v_t_sb[:, i, :], ident_f32[:])
+            nc.scalar.copy(out=out_blk[:, 2, :, :], in_=v_back[:])
+
         def finish_v_block(v, out_blk):
             nc.vector.tensor_tensor(
                 out=out_blk[:, 2, :, :],
@@ -281,6 +307,7 @@ def tile_arlowvisionattention_pa_t_kernel(
             )
 
         grouped_tiles, quantised, projected, turned_back, out_blks = {}, {}, {}, {}, {}
+        v_transposed = {}
 
         def store(outputs, first, count):
             place = first % BLOCK
@@ -290,10 +317,17 @@ def tile_arlowvisionattention_pa_t_kernel(
                     in_=out_blks[first // BLOCK][:, j, place : place + count, :],
                 )
 
+        def project_last_v():
+            v = psum_v.tile([P, BLOCK, V], F32, name="v")
+            for r in (ROUNDS - 2, ROUNDS - 1):
+                project_v_round(r, quantised[r], v)
+            return empty_v_block(v)
+
         prepare_weights()
         nc.vector.tensor_copy(
-            out=bias_sorted[:], in_=bias_row[:, 0:QK].rearrange("p (n e) -> p e n", e=2)
+            out=bias_sorted[:, 0:2, :], in_=bias_row[:, 0:QK].rearrange("p (n e) -> p e n", e=2)
         )
+        nc.vector.tensor_copy(out=bias_sorted[:, 2, :], in_=bias_row[:, QK : QK + V])
 
         for a in range(-4, ROUNDS, 2):
             for r in (a, a + 1):
@@ -301,14 +335,22 @@ def tile_arlowvisionattention_pa_t_kernel(
                     grouped_tiles[r + 4] = transpose_round(r + 4)
                 if r >= 0:
                     turned_back[r] = turn_back_round(projected[r])
+                if r == ROUNDS - 2:
+                    v_transposed[BLOCKS - 1] = project_last_v()
                 if r == -2:
                     spread_bias()
                 if 0 <= r + 2 < ROUNDS:
                     projected[r + 2] = project_qk_round(quantised[r + 2])
-            if 0 <= a + 2 < ROUNDS:
+            block = a * ROUND // BLOCK
+            if block in v_transposed:
+                turn_back_v_block(v_transposed[block], out_blks[block])
+                store(range(2, 3), a * ROUND, BLOCK)
+            if 0 <= a + 2 < ROUNDS - 2:
                 v = psum_v.tile([P, BLOCK, V], F32, name="v")
                 for r in (a + 2, a + 3):
                     project_v_round(r, quantised[r], v)
+                if block + 1 >= BLOCKS - V_TURNED:
+                    v_transposed[block + 1] = empty_v_block(v)
                 if a + 6 < ROUNDS:
                     sort_tile((a + 8) * ROUND - 1)
             if a * ROUND in TABLE_PARTS:
@@ -321,11 +363,12 @@ def tile_arlowvisionattention_pa_t_kernel(
                 if r >= 0:
                     engine = nc.vector if r == ROUNDS - 1 else nc.gpsimd
                     finish_qk_round(engine, r, by_cos, by_sin, out_blks[r * ROUND // BLOCK])
-                    if a == ROUNDS - 2:
+                    if block >= BLOCKS - 2:
                         store(range(2), r * ROUND, ROUND)
             if 0 <= a + 2 < ROUNDS:
                 out_blks[(a + 2) * ROUND // BLOCK] = out_pool.tile([P, 3, BLOCK, V], F32, name="out_blk")
-                finish_v_block(v, out_blks[(a + 2) * ROUND // BLOCK])
-                store(range(2, 3), (a + 2) * ROUND, BLOCK)
-            if 0 <= a < ROUNDS - 2:
+                if block + 1 < BLOCKS - V_TURNED:
+                    finish_v_block(v, out_blks[block + 1])
+                    store(range(2, 3), (a + 2) * ROUND, BLOCK)
+            if 0 <= block < BLOCKS - 2:
                 store(range(2), a * ROUND, BLOCK)

from contextlib import ExitStack

import concourse.mybir as mybir
from concourse.masks import make_identity

F32 = mybir.dt.float32
BF16 = mybir.dt.bfloat16
U32 = mybir.dt.uint32
U8 = mybir.dt.uint8
FP8X4 = mybir.dt.float8_e4m3fn_x4
MULT = mybir.AluOpType.mult
ADD = mybir.AluOpType.add
IDENTITY = mybir.ActivationFunctionType.Identity

P = 128
PACK = 4
TOKENS = 8192
HIDDEN = 1024
HEAD_DIM = 32
PAIRS = HEAD_DIM // 2
QK_HEADS = 8
QK = QK_HEADS * HEAD_DIM
HALF = QK // 2
V = 4 * HEAD_DIM
BANK = 512
PASSES = HIDDEN // (P * PACK)
WORD_BLOCKS = HIDDEN // (2 * P)
TILES = TOKENS // P
ROUND = 2
ROUNDS = TILES // ROUND
BLOCK = 4
BLOCKS = TILES // BLOCK
X_BUFS = 3
FIRST_BLOCKS = 2
V_TURNED = 2
FIRST_TILES = FIRST_BLOCKS * BLOCK
TABLE_PARTS = {0: 16, 16: TILES}

FLOPS = 2 * TOKENS * HIDDEN * (QK + V)


def tile_arlowvisionattention_pa_t_kernel(
    tc, hidden_states, cos, sin, w_qkv, b_qkv, out_0, out_1, out_2
):
    nc = tc.nc
    x_view = hidden_states.rearrange("(p m) k -> p m k", m=TILES)
    out_views = [o.rearrange("(p m) h d -> p m (h d)", m=TILES) for o in (out_0, out_1, out_2)]

    with ExitStack() as ctx:
        const = ctx.enter_context(tc.tile_pool(name="const", bufs=1))
        x_first_pool = ctx.enter_context(tc.tile_pool(name="x_first", bufs=FIRST_TILES))
        x_pool = ctx.enter_context(tc.tile_pool(name="x", bufs=X_BUFS))
        sort_pool = ctx.enter_context(tc.tile_pool(name="sort", bufs=2))
        mx_pool = ctx.enter_context(tc.tile_pool(name="mx", bufs=5))
        rope_pool = ctx.enter_context(tc.tile_pool(name="rope", bufs=4))
        out_pool = ctx.enter_context(tc.tile_pool(name="out", bufs=4))
        psum_x = ctx.enter_context(tc.psum_pool(name="psum_x", bufs=3))
        psum_qk_t = ctx.enter_context(tc.psum_pool(name="psum_qk_t", bufs=2))
        psum_qk = ctx.enter_context(tc.psum_pool(name="psum_qk", bufs=2))
        psum_v = ctx.enter_context(tc.psum_pool(name="psum_v", bufs=1))
        ctx.enter_context(tc.manual_schedule())

        x_tiles = {}

        def load_tiles(pool, name, first, count):
            x_sb = pool.tile([P, count, HIDDEN], BF16, name=name)
            nc.sync.dma_start(out=x_sb[:], in_=x_view[:, first : first + count, :])
            for i in range(count):
                x_tiles[first + i] = (x_sb, i)

        cos_sb = const.tile([P, TILES, HEAD_DIM], BF16, name="cos_sb")
        sin_sb = const.tile([P, TILES, HEAD_DIM], BF16, name="sin_sb")

        def load_tables(first, last):
            for table_sb, table in ((cos_sb, cos), (sin_sb, sin)):
                nc.sync.dma_start(
                    out=table_sb[:, first:last, :],
                    in_=table.rearrange("(p m) d -> p m d", m=TILES)[:, first:last, :],
                )

        bias_row = const.tile([P, BANK], BF16, name="bias_row")
        nc.vector.memset(bias_row[:], 0.0)
        w_raw = const.tile([P, PASSES, PACK, QK + V], BF16, name="w_raw")
        nc.sync.dma_start(
            out=w_raw[:], in_=w_qkv.rearrange("(g p t) c -> p g t c", g=PASSES, t=PACK)
        )
        nc.sync.dma_start(
            out=bias_row[0:1, 0 : QK + V], in_=b_qkv.rearrange("(o n) -> o n", o=1)
        )
        for i in range(FIRST_TILES):
            load_tiles(x_first_pool, "x_tile", i, 1)
        load_tables(0, TABLE_PARTS[0])
        for b in range(FIRST_BLOCKS, FIRST_BLOCKS + X_BUFS):
            load_tiles(x_pool, "x_blk", b * BLOCK, BLOCK)
        load_tables(TABLE_PARTS[0], TILES)

        ident_f32 = const.tile([P, P], F32, name="ident_f32")
        make_identity(nc, ident_f32[:])
        ident_bf16 = const.tile([P, P], BF16, name="ident_bf16")
        make_identity(nc, ident_bf16[:])

        ones = const.tile([P, P], BF16, name="ones")
        nc.vector.memset(ones[:], 1.0)
        bias_v = const.tile([P, V], BF16, name="bias_v")
        bias_sorted = const.tile([P, 3, P], BF16, name="bias_sorted")
        bias_cols = const.tile([P, 3], F32, name="bias_cols")

        def spread_bias():
            bias_spread = psum_qk.tile([P, BANK], F32, name="bias_spread", tag="qk")
            nc.tensor.matmul(out=bias_spread[:], lhsT=ones[:], rhs=bias_row[:], start=True, stop=True)
            nc.scalar.copy(out=bias_v[:], in_=bias_spread[:, QK : QK + V])
            bias_sorted_t = psum_x.tile([P, 3, P], BF16, name="bias_sorted_t", tag="x_t")
            for e in range(3):
                nc.tensor.transpose(bias_sorted_t[:, e, :], bias_sorted[:, e, :], ident_bf16[:])
            nc.scalar.copy(out=bias_cols[:], in_=bias_sorted_t[:, :, 0])

        w_qk_grouped = const.tile([P, PASSES, 2, HALF, PACK], BF16, name="w_qk_grouped", align_bytes=64)
        w_v_grouped = const.tile([P, PASSES, V, PACK], BF16, name="w_v_grouped", align_bytes=64)
        w_qk_codes = const.tile([P, PASSES, 2, HALF], U32, name="w_qk_codes", align_bytes=64)
        w_qk_scales = const.tile([P, PASSES, 2, HALF], U8, name="w_qk_scales", align_bytes=64)
        w_v_codes = const.tile([P, PASSES, V], U32, name="w_v_codes", align_bytes=64)
        w_v_scales = const.tile([P, PASSES, V], U8, name="w_v_scales", align_bytes=64)

        def prepare_weights():
            w_rows = w_raw[:]
            w_halves = w_rows[:, :, :, 0:QK].rearrange("p g t (n e) -> p e g n t", e=2)
            nc.vector.tensor_copy(out=w_qk_grouped[:, :, 0], in_=w_halves[:, 0])
            nc.scalar.copy(out=w_qk_grouped[:, :, 1], in_=w_halves[:, 1])
            nc.vector.tensor_copy(
                out=w_v_grouped[:], in_=w_rows[:, :, :, QK : QK + V].rearrange("p g t n -> p g n t")
            )
            nc.vector.quantize_mx(
                out=w_qk_codes[:].rearrange("p g e n -> p (g e n)").bitcast(FP8X4),
                scales=w_qk_scales[:].rearrange("p g e n -> p (g e n)"),
                in_=w_qk_grouped[:].rearrange("p g e n t -> p (g e n t)"),
            )
            nc.vector.quantize_mx(
                out=w_v_codes[:].rearrange("p g n -> p (g n)").bitcast(FP8X4),
                scales=w_v_scales[:].rearrange("p g n -> p (g n)"),
                in_=w_v_grouped[:].rearrange("p g n t -> p (g n t)"),
            )

        signs = const.tile([P, HEAD_DIM], BF16, name="signs")
        nc.vector.memset(signs[:], 1.0)
        nc.vector.memset(signs[:].rearrange("p (i e) -> p i e", e=2)[:, :, 0], -1.0)

        def sign_sin(first, last):
            nc.vector.tensor_tensor(
                out=sin_sb[:, first:last, :],
                in0=sin_sb[:, first:last, :],
                in1=signs[:].unsqueeze(1).to_broadcast([P, last - first, HEAD_DIM]),
                op=MULT,
            )

        sorted_tiles = {}

        def sort_tile(tile_index):
            x_sb, place = x_tiles[tile_index]
            x_sorted = sort_pool.tile([P, PASSES, 2, P], F32, name="x_sorted")
            nc.scalar.copy(
                out=x_sorted[:].rearrange("p g u w -> p g w u"),
                in_=x_sb[:, place, :].bitcast(F32).rearrange("p (g w u) -> p g w u", g=PASSES, u=2),
            )
            sorted_tiles[tile_index] = x_sorted

        def transpose_round(r):
            grouped = mx_pool.tile([P, PASSES, ROUND, P, PACK], BF16, name="grouped", align_bytes=64)
            grouped_words = grouped[:].bitcast(F32)
            for a in range(ROUND):
                x_sb, place = x_tiles[r * ROUND + a]
                words = x_sb[:, place, :].bitcast(F32)
                x_sorted = sorted_tiles.get(r * ROUND + a)
                x_t = psum_x.tile([P, WORD_BLOCKS, P], F32, name="x_t", tag="x_t")
                for j in range(WORD_BLOCKS):
                    g, u = divmod(j, 2)
                    if x_sorted is None:
                        every_2nd = words[:, 2 * P * g + u : 2 * P * (g + 1) : 2]
                    else:
                        every_2nd = x_sorted[:, g, u, :]
                    nc.tensor.transpose(x_t[:, j, :], every_2nd, ident_f32[:])
                nc.scalar.copy(
                    out=grouped_words[:, :, a], in_=x_t[:].rearrange("p (g u) r -> p g r u", u=2)
                )
            b = r * ROUND // BLOCK
            if (r + 1) * ROUND % BLOCK == 0 and FIRST_BLOCKS <= b < BLOCKS - X_BUFS:
                load_tiles(x_pool, "x_blk", (b + X_BUFS) * BLOCK, BLOCK)
            return grouped

        def quantise_round(grouped):
            codes = mx_pool.tile([P, PASSES, ROUND, P], U32, name="codes", align_bytes=64)
            scales = mx_pool.tile([P, PASSES, ROUND, P], U8, name="scales", align_bytes=64)
            nc.vector.quantize_mx(
                out=codes[:].rearrange("p g a r -> p (g a r)").bitcast(FP8X4),
                scales=scales[:].rearrange("p g a r -> p (g a r)"),
                in_=grouped[:].rearrange("p g a r t -> p (g a r t)"),
            )
            return codes, scales

        def project_qk_round(codes_and_scales):
            codes, scales = codes_and_scales
            qk_t = psum_qk_t.tile([P, 2, ROUND * P], F32, name="qk_t")
            for e in range(2):
                for g in range(PASSES):
                    nc.tensor.matmul_mx(
                        out=qk_t[:, e, :],
                        lhsT=w_qk_codes[:, g, e, :].bitcast(FP8X4),
                        lhsT_scale=w_qk_scales[:, g, e, :],
                        rhs=codes[:, g].rearrange("p a r -> p (a r)").bitcast(FP8X4),
                        rhs_scale=scales[:, g].rearrange("p a r -> p (a r)"),
                        start=(g == 0),
                        stop=(g == PASSES - 1),
                    )
            qk_t_sb = rope_pool.tile([P, 2, ROUND * P], F32, name="qk_t_sb")
            for e in range(2):
                nc.scalar.activation(
                    out=qk_t_sb[:, e, :],
                    in_=qk_t[:, e, :],
                    func=IDENTITY,
                    bias=bias_cols[:, e : e + 1],
                    scale=1.0,
                )
            return qk_t_sb

        def project_v_round(r, codes_and_scales, v):
            codes, scales = codes_and_scales
            if r * ROUND // BLOCK >= BLOCKS - V_TURNED:
                for g in range(PASSES):
                    nc.tensor.matmul_mx(
                        out=v[:, r * ROUND % BLOCK : r * ROUND % BLOCK + ROUND, :].rearrange("p a c -> p (a c)"),
                        lhsT=w_v_codes[:, g, :].bitcast(FP8X4),
                        lhsT_scale=w_v_scales[:, g, :],
                        rhs=codes[:, g].rearrange("p a r -> p (a r)").bitcast(FP8X4),
                        rhs_scale=scales[:, g].rearrange("p a r -> p (a r)"),
                        start=(g == 0),
                        stop=(g == PASSES - 1),
                    )
                return
            for a in range(ROUND):
                for g in range(PASSES):
                    nc.tensor.matmul_mx(
                        out=v[:, r * ROUND % BLOCK + a, :],
                        lhsT=codes[:, g, a, :].bitcast(FP8X4),
                        lhsT_scale=scales[:, g, a, :],
                        rhs=w_v_codes[:, g, :].bitcast(FP8X4),
                        rhs_scale=w_v_scales[:, g, :],
                        start=(g == 0),
                        stop=(g == PASSES - 1),
                    )

        def turn_back_round(qk_t_sb):
            qk = psum_qk.tile([P, ROUND, 2, HALF], F32, name="qk", tag="qk")
            for a in range(ROUND):
                for e in range(2):
                    nc.tensor.transpose(
                        qk[:, a, e, :], qk_t_sb[:, e, a * P : (a + 1) * P], ident_f32[:]
                    )
            return qk

        def multiply_round(r, qk):
            shape = [P, ROUND, QK_HEADS, PAIRS, 2]
            tiles = slice(r * ROUND, (r + 1) * ROUND)
            halves = qk[:].rearrange("p a e (h i) -> p a e h i", i=PAIRS)
            by_cos = rope_pool.tile(shape, F32, name="by_cos")
            nc.vector.tensor_tensor(
                out=by_cos[:],
                in0=halves.rearrange("p a e h i -> p a h i e"),
                in1=cos_sb[:, tiles, :].rearrange("p a (i e) -> p a i e", e=2).unsqueeze(2).to_broadcast(shape),
                op=MULT,
            )
            by_sin = rope_pool.tile(shape, F32, name="by_sin")
            nc.vector.tensor_tensor(
                out=by_sin[:],
                in0=halves[:, :, ::-1].rearrange("p a e h i -> p a h i e"),
                in1=sin_sb[:, tiles, :].rearrange("p a (i e) -> p a i e", e=2).unsqueeze(2).to_broadcast(shape),
                op=MULT,
            )
            return by_cos, by_sin

        def finish_qk_round(engine, r, by_cos, by_sin, out_blk):
            first = r * ROUND % BLOCK
            engine.tensor_tensor(
                out=out_blk[:, 0:2, first : first + ROUND, :].rearrange("p j a c -> p a j c"),
                in0=by_cos[:].rearrange("p a (j h) i e -> p a j (h i e)", j=2),
                in1=by_sin[:].rearrange("p a (j h) i e -> p a j (h i e)", j=2),
                op=ADD,
            )

        def empty_v_block(v):
            v_t_sb = rope_pool.tile([P, BLOCK, P], F32, name="v_t_sb")
            nc.scalar.activation(
                out=v_t_sb[:], in_=v[:], func=IDENTITY, bias=bias_cols[:, 2:3], scale=1.0
            )
            return v_t_sb

        def turn_back_v_block(v_t_sb, out_blk):
            v_back = psum_x.tile([P, BLOCK, P], F32, name="v_back", tag="x_t")
            for i in range(BLOCK):
                nc.tensor.transpose(v_back[:, i, :], v_t_sb[:, i, :], ident_f32[:])
            nc.scalar.copy(out=out_blk[:, 2, :, :], in_=v_back[:])

        def finish_v_block(v, out_blk):
            nc.vector.tensor_tensor(
                out=out_blk[:, 2, :, :],
                in0=v[:],
                in1=bias_v[:].unsqueeze(1).to_broadcast([P, BLOCK, V]),
                op=ADD,
            )

        grouped_tiles, quantised, projected, turned_back, out_blks = {}, {}, {}, {}, {}
        v_transposed = {}

        def store(outputs, first, count):
            place = first % BLOCK
            for j in outputs:
                nc.sync.dma_start(
                    out=out_views[j][:, first : first + count, :],
                    in_=out_blks[first // BLOCK][:, j, place : place + count, :],
                )

        def project_last_v():
            v = psum_v.tile([P, BLOCK, V], F32, name="v")
            for r in (ROUNDS - 2, ROUNDS - 1):
                project_v_round(r, quantised[r], v)
            return empty_v_block(v)

        prepare_weights()
        nc.vector.tensor_copy(
            out=bias_sorted[:, 0:2, :], in_=bias_row[:, 0:QK].rearrange("p (n e) -> p e n", e=2)
        )
        nc.vector.tensor_copy(out=bias_sorted[:, 2, :], in_=bias_row[:, QK : QK + V])

        for a in range(-4, ROUNDS, 2):
            for r in (a, a + 1):
                if r + 4 < ROUNDS:
                    grouped_tiles[r + 4] = transpose_round(r + 4)
                if r >= 0:
                    turned_back[r] = turn_back_round(projected[r])
                if r == ROUNDS - 2:
                    v_transposed[BLOCKS - 1] = project_last_v()
                if r == -2:
                    spread_bias()
                if 0 <= r + 2 < ROUNDS:
                    projected[r + 2] = project_qk_round(quantised[r + 2])
            block = a * ROUND // BLOCK
            if block in v_transposed:
                turn_back_v_block(v_transposed[block], out_blks[block])
                store(range(2, 3), a * ROUND, BLOCK)
            if 0 <= a + 2 < ROUNDS - 2:
                v = psum_v.tile([P, BLOCK, V], F32, name="v")
                for r in (a + 2, a + 3):
                    project_v_round(r, quantised[r], v)
                if block + 1 >= BLOCKS - V_TURNED:
                    v_transposed[block + 1] = empty_v_block(v)
                if a + 6 < ROUNDS:
                    sort_tile((a + 8) * ROUND - 1)
            if a * ROUND in TABLE_PARTS:
                sign_sin(a * ROUND, TABLE_PARTS[a * ROUND])
            for r in (a, a + 1):
                if r >= 0:
                    by_cos, by_sin = multiply_round(r, turned_back[r])
                if r + 4 < ROUNDS:
                    quantised[r + 4] = quantise_round(grouped_tiles[r + 4])
                if r >= 0:
                    engine = nc.vector if r == ROUNDS - 1 else nc.gpsimd
                    finish_qk_round(engine, r, by_cos, by_sin, out_blks[r * ROUND // BLOCK])
                    if block >= BLOCKS - 2:
                        store(range(2), r * ROUND, ROUND)
            if 0 <= a + 2 < ROUNDS:
                out_blks[(a + 2) * ROUND // BLOCK] = out_pool.tile([P, 3, BLOCK, V], F32, name="out_blk")
                if block + 1 < BLOCKS - V_TURNED:
                    finish_v_block(v, out_blks[block + 1])
                    store(range(2, 3), (a + 2) * ROUND, BLOCK)
            if 0 <= block < BLOCKS - 2:
                store(range(2), a * ROUND, BLOCK)
